import numpy as np
import ml_dtypes


def mxq(x, axis, fmt="e4m3"):
    dtype, down = {"e4m3": (ml_dtypes.float8_e4m3fn, 7), "e5m2": (ml_dtypes.float8_e5m2, 14)}[fmt]
    v = np.moveaxis(np.asarray(x, np.float32).astype(ml_dtypes.bfloat16).astype(np.float64), axis, -1)
    blocks = v.reshape(v.shape[:-1] + (-1, 32))
    amax = np.abs(blocks).max(-1, keepdims=True)
    byte = np.maximum(np.where(amax > 0, np.frexp(amax)[1] - 1 + 127, 0) - down, 1)
    scale = np.exp2(byte - 127.0)
    codes = (blocks / scale).astype(np.float32).astype(dtype).astype(np.float64)
    return np.moveaxis((codes * scale).reshape(v.shape), -1, axis)


WIDE = False


def mx_kscale(k):
    if not WIDE:
        return np.ones(k)
    levels = np.array([10, -10, 5, -5, 0])
    a = np.random.permutation(np.resize(levels, k // 512 * 4)).reshape(k // 512, 4)
    idx = np.arange(k)
    return np.exp2(a[idx // 512, idx % 128 // 32])


BF16 = ml_dtypes.bfloat16


def bf(x):
    return np.asarray(x, np.float32).astype(BF16)


def f64(x):
    return np.asarray(x).astype(np.float64)


B, DIN, NU, N, ORDER = 1, 128, 128, 512, 3
C = DIN + NU
KC = (ORDER + 1) * C


def sigmoid(v):
    return 1.0 / (1.0 + np.exp(-v))


def setup_inputs():
    sb = np.array(mx_kscale(KC)).reshape(ORDER + 1, C)
    sb[0, DIN:] = 1.0
    sb[ORDER] = sb[ORDER - 1]
    s = sb.reshape(KC)
    return {"x": bf(np.random.standard_normal((B, DIN, N)) * sb[0, :DIN, None]),
            "h_dn": bf(np.random.standard_normal((B, NU, N)) * 0.6),
            "xg1": bf(np.random.standard_normal((B, C, N)) * 0.75 * sb[1][:, None]),
            "xg2": bf(np.random.standard_normal((B, C, N)) * 0.75 * sb[ORDER - 1][:, None]),
            "adj": bf(np.random.standard_normal((N, N)) / np.sqrt(N)),
            "W_u": bf(np.random.standard_normal((NU, KC)) / np.sqrt(KC) / s),
            "b_u": bf(np.random.standard_normal(NU) * 0.2),
            "W_c": bf(np.random.standard_normal((NU, KC)) / np.sqrt(KC) / s),
            "b_c": bf(np.random.standard_normal(NU) * 0.2)}


def reference(x, h_dn, xg1, xg2, adj, W_u, b_u, W_c, b_c):
    hd = f64(h_dn)
    x2 = f64(xg2)
    xg3 = mxq(x2, 2, "e4m3") @ mxq(f64(adj), 1, "e4m3").T
    z = np.concatenate([f64(x), hd, f64(xg1), x2, xg3], axis=1)
    zq = mxq(z, 1, "e4m3")
    u = sigmoid((mxq(f64(W_u), 1, "e4m3") @ zq) + f64(b_u)[None, :, None])
    c = np.tanh((mxq(f64(W_c), 1, "e4m3") @ zq) + f64(b_c)[None, :, None])
    return u * hd + (1.0 - u) * c

@@ -1,0 +1,196 @@
+from contextlib import ExitStack
+
+import concourse.masks as masks
+import concourse.mybir as mybir
+
+F32 = mybir.dt.float32
+BF16 = mybir.dt.bfloat16
+U32 = mybir.dt.uint32
+U8 = mybir.dt.uint8
+FP8X4 = mybir.dt.float8_e4m3fn_x4
+ACT = mybir.ActivationFunctionType
+ALU = mybir.AluOpType
+
+P = 128
+NODES = 512
+HALF = NODES // 2
+QUARTER = NODES // 4
+KC = 1024
+
+FLOPS = 2 * 256 * NODES * NODES + 2 * 2 * P * KC * NODES
+
+
+def mx_operand(pool, name, columns):
+    grouped = pool.tile([P, 4 * columns], BF16, name=name + "_grouped", align_bytes=64)
+    codes = pool.tile([P, columns], U32, name=name + "_codes", align_bytes=64)
+    scales = pool.tile([P, columns], U8, name=name + "_scales", align_bytes=64)
+    return grouped, codes, scales
+
+
+def quantise(nc, operand, first, count):
+    grouped, codes, scales = operand
+    nc.vector.quantize_mx(
+        out=codes[:, first : first + count].bitcast(FP8X4),
+        scales=scales[:, first : first + count],
+        in_=grouped[:, 4 * first : 4 * (first + count)],
+    )
+
+
+def flip(nc, bank, blocks, ident):
+    for s in range(4):
+        nc.tensor.transpose(bank[:, s, :], blocks[s], ident[:])
+
+
+def interleave(copy, operand, bank):
+    grouped = operand[0]
+    copy(
+        out=grouped[:].bitcast(F32).rearrange("p (a m u) -> p a m u", a=2, u=2),
+        in_=bank[:].rearrange("p (a u) m -> p a m u", u=2),
+    )
+
+
+def tile_gcgrucell_epsilon_pb_s_kernel(tc, x, h_dn, xg1, xg2, adj, W_u, b_u, W_c, b_c, out):
+    nc = tc.nc
+    with ExitStack() as ctx:
+        sbuf = ctx.enter_context(tc.tile_pool(name="sbuf", bufs=1))
+        joined = ctx.enter_context(tc.psum_pool(name="joined", bufs=1))
+        work = ctx.enter_context(tc.psum_pool(name="work", bufs=4))
+
+        ident_f32 = sbuf.tile([P, P], F32, name="ident_f32")
+        masks.make_identity(nc, ident_f32[:])
+        ident_bf16 = sbuf.tile([P, P], BF16, name="ident_bf16")
+        masks.make_identity(nc, ident_bf16[:])
+        warm_in = sbuf.tile([P, 1], F32, name="warm_in")
+        warm_out = sbuf.tile([P, 1], F32, name="warm_out")
+        nc.vector.memset(warm_in[:], 0.0)
+        nc.scalar.activation(out=warm_out[:], in_=warm_in[:], func=ACT.Sigmoid)
+
+        bias = []
+        for g, b in enumerate((b_u, b_c)):
+            col = sbuf.tile([P, 1], BF16, name="bias%d" % g)
+            nc.scalar.dma_start(out=col[:], in_=b.rearrange("(p o) -> p o", o=1))
+            bias.append(col)
+        xg2_rows = sbuf.tile([P, 2 * NODES], BF16, name="xg2_rows")
+        nc.sync.dma_start(out=xg2_rows[:], in_=xg2.rearrange("b (p j) v -> p (b j v)", j=2))
+        adj_rows = []
+        for h in range(2):
+            rows = sbuf.tile([P, 2 * NODES], BF16, name="adj_rows%d" % h)
+            nc.sync.dma_start(
+                out=rows[:].rearrange("p (i v) -> p i v", i=2),
+                in_=adj[HALF * h : HALF * (h + 1), :].rearrange("(i p) v -> p i v", p=P),
+            )
+            adj_rows.append(rows)
+        early_rows = sbuf.tile([P, 4 * NODES], BF16, name="early_rows")
+        nc.sync.dma_start(out=early_rows[0:32, :], in_=x.rearrange("b (p j) n -> p (b j n)", j=4))
+        nc.sync.dma_start(out=early_rows[32:64, :], in_=h_dn.rearrange("b (p j) n -> p (b j n)", j=4))
+        nc.sync.dma_start(out=early_rows[64:128, :], in_=xg1.rearrange("b (p j) n -> p (b j n)", j=4))
+        w_rows = []
+        for g, w in enumerate((W_u, W_c)):
+            rows = sbuf.tile([P, KC], BF16, name="w_rows%d" % g)
+            nc.sync.dma_start(out=rows[:], in_=w)
+            w_rows.append(rows)
+        h_rows = sbuf.tile([P, NODES], BF16, name="h_rows")
+        nc.sync.dma_start(out=h_rows[:], in_=h_dn.rearrange("b o n -> (b o) n"))
+
+        xg2_t = mx_operand(sbuf, "xg2_t", 2 * P)
+        xg2_words = xg2_rows[:].bitcast(F32)
+        bank = work.tile([P, 4, P], F32, name="xg2_bank", tag="work")
+        flip(nc, bank, [xg2_words[:, P * s : P * (s + 1)] for s in range(4)], ident_f32)
+        interleave(nc.scalar.copy, xg2_t, bank)
+        quantise(nc, xg2_t, 0, 2 * P)
+
+        z1_bank = []
+        for q in range(4):
+            zb = joined.tile([P, 4, QUARTER], F32, name="z1_bank%d" % q)
+            for j in range(2):
+                nc.tensor.matmul(
+                    out=zb[:, j, :],
+                    lhsT=ident_bf16[:],
+                    rhs=xg2_rows[:, NODES * j + QUARTER * q : NODES * j + QUARTER * (q + 1)],
+                    start=True,
+                    stop=True,
+                )
+            z1_bank.append(zb)
+
+        adj_t = []
+        for h in range(2):
+            operand = mx_operand(sbuf, "adj_t%d" % h, HALF)
+            adj_words = adj_rows[h][:].bitcast(F32)
+            bank = work.tile([P, 4, P], F32, name="adj_bank%d" % h, tag="work")
+            flip(nc, bank, [adj_words[:, P * s : P * (s + 1)] for s in range(4)], ident_f32)
+            interleave(nc.scalar.copy, operand, bank)
+            quantise(nc, operand, 0, HALF)
+            adj_t.append(operand)
+
+        z0 = mx_operand(sbuf, "z0", NODES)
+        nc.vector.tensor_copy(
+            out=z0[0][:].rearrange("p (c i t) -> p c t i", i=4, t=4),
+            in_=early_rows[:].rearrange("p (t c i) -> p c t i", t=4, i=4),
+        )
+        quantise(nc, z0, 0, NODES)
+
+        w_t = []
+        for g in range(2):
+            operand = mx_operand(sbuf, "w_t%d" % g, 2 * P)
+            w_words = w_rows[g][:].bitcast(F32)
+            blocks = [w_words[:, 0:256:2], w_words[:, 1:256:2], w_words[:, 256:384], w_words[:, 384:512]]
+            bank = work.tile([P, 4, P], F32, name="w_bank%d" % g, tag="work")
+            flip(nc, bank, blocks, ident_f32)
+            interleave(nc.scalar.copy, operand, bank)
+            quantise(nc, operand, 0, 2 * P)
+            w_t.append(operand)
+
+        for q in range(4):
+            cols = slice(QUARTER * (q % 2), QUARTER * (q % 2 + 1))
+            for j in range(2):
+                nc.tensor.matmul_mx(
+                    out=z1_bank[q][:, 2 + j, :],
+                    lhsT=xg2_t[1][:, P * j : P * (j + 1)].bitcast(FP8X4),
+                    lhsT_scale=xg2_t[2][:, P * j : P * (j + 1)],
+                    rhs=adj_t[q // 2][1][:, cols].bitcast(FP8X4),
+                    rhs_scale=adj_t[q // 2][2][:, cols],
+                    start=True,
+                    stop=True,
+                )
+
+        def gate_pass(acc, g, k_pass, operand, h):
+            nc.tensor.matmul_mx(
+                out=acc[:],
+                lhsT=w_t[g][1][:, P * k_pass : P * (k_pass + 1)].bitcast(FP8X4),
+                lhsT_scale=w_t[g][2][:, P * k_pass : P * (k_pass + 1)],
+                rhs=operand[1][:, HALF * h : HALF * (h + 1)].bitcast(FP8X4),
+                rhs_scale=operand[2][:, HALF * h : HALF * (h + 1)],
+                start=(k_pass == 0),
+                stop=(k_pass == 1),
+            )
+
+        gate = {}
+        for h in range(2):
+            for g in range(2):
+                gate[g, h] = work.tile([P, HALF], F32, name="gate%d%d" % (g, h), tag="work")
+                gate_pass(gate[g, h], g, 0, z0, h)
+
+        z1 = mx_operand(sbuf, "z1", NODES)
+        out_rows = out.rearrange("b o n -> (b o) n")
+        for h in range(2):
+            for q in (2 * h, 2 * h + 1):
+                copy = nc.scalar.copy if q % 2 == 0 else nc.vector.tensor_copy
+                copy(
+                    out=z1[0][:, 4 * QUARTER * q : 4 * QUARTER * (q + 1)].rearrange("p (n t) -> p n t", t=4),
+                    in_=z1_bank[q][:].rearrange("p t n -> p n t"),
+                )
+            quantise(nc, z1, HALF * h, HALF)
+            for g in (1, 0):
+                gate_pass(gate[g, h], g, 1, z1, h)
+            cols = slice(HALF * h, HALF * (h + 1))
+            cand = sbuf.tile([P, HALF], F32, name="cand%d" % h)
+            nc.scalar.activation(out=cand[:], in_=gate[1, h][:], func=ACT.Tanh, bias=bias[1][:], scale=1.0)
+            upd = sbuf.tile([P, HALF], F32, name="upd%d" % h)
+            nc.scalar.activation(out=upd[:], in_=gate[0, h][:], func=ACT.Sigmoid, bias=bias[0][:], scale=1.0)
+            diff = sbuf.tile([P, HALF], F32, name="diff%d" % h)
+            nc.vector.tensor_tensor(out=diff[:], in0=h_rows[:, cols], in1=cand[:], op=ALU.subtract)
+            prod = sbuf.tile([P, HALF], F32, name="prod%d" % h)
+            nc.vector.tensor_tensor(out=prod[:], in0=upd[:], in1=diff[:], op=ALU.mult)
+            res = sbuf.tile([P, HALF], F32, name="res%d" % h)
+            nc.vector.tensor_tensor(out=res[:], in0=prod[:], in1=cand[:], op=ALU.add)
+            nc.sync.dma_start(out=out_rows[:, cols], in_=res[:])

@@ -53,23 +53,16 @@ def tile_gcgrucell_epsilon_pb_s_kernel(tc, x, h_dn, xg1, xg2, adj, W_u, b_u, W_c
     nc = tc.nc
     with ExitStack() as ctx:
         sbuf = ctx.enter_context(tc.tile_pool(name="sbuf", bufs=1))
-        joined = ctx.enter_context(tc.psum_pool(name="joined", bufs=1))
+        hop_psum = ctx.enter_context(tc.psum_pool(name="hop_psum", bufs=1))
         work = ctx.enter_context(tc.psum_pool(name="work", bufs=4))
 
         ident_f32 = sbuf.tile([P, P], F32, name="ident_f32")
         masks.make_identity(nc, ident_f32[:])
-        ident_bf16 = sbuf.tile([P, P], BF16, name="ident_bf16")
-        masks.make_identity(nc, ident_bf16[:])
         warm_in = sbuf.tile([P, 1], F32, name="warm_in")
         warm_out = sbuf.tile([P, 1], F32, name="warm_out")
         nc.vector.memset(warm_in[:], 0.0)
         nc.scalar.activation(out=warm_out[:], in_=warm_in[:], func=ACT.Sigmoid)
 
-        bias = []
-        for g, b in enumerate((b_u, b_c)):
-            col = sbuf.tile([P, 1], BF16, name="bias%d" % g)
-            nc.scalar.dma_start(out=col[:], in_=b.rearrange("(p o) -> p o", o=1))
-            bias.append(col)
         xg2_rows = sbuf.tile([P, 2 * NODES], BF16, name="xg2_rows")
         nc.sync.dma_start(out=xg2_rows[:], in_=xg2.rearrange("b (p j) v -> p (b j v)", j=2))
         adj_rows = []
@@ -81,9 +74,9 @@ def tile_gcgrucell_epsilon_pb_s_kernel(tc, x, h_dn, xg1, xg2, adj, W_u, b_u, W_c
             )
             adj_rows.append(rows)
         early_rows = sbuf.tile([P, 4 * NODES], BF16, name="early_rows")
+        nc.scalar.dma_start(out=early_rows[64:128, :], in_=xg1.rearrange("b (p j) n -> p (b j n)", j=4))
         nc.sync.dma_start(out=early_rows[0:32, :], in_=x.rearrange("b (p j) n -> p (b j n)", j=4))
         nc.sync.dma_start(out=early_rows[32:64, :], in_=h_dn.rearrange("b (p j) n -> p (b j n)", j=4))
-        nc.sync.dma_start(out=early_rows[64:128, :], in_=xg1.rearrange("b (p j) n -> p (b j n)", j=4))
         w_rows = []
         for g, w in enumerate((W_u, W_c)):
             rows = sbuf.tile([P, KC], BF16, name="w_rows%d" % g)
@@ -91,26 +84,27 @@ def tile_gcgrucell_epsilon_pb_s_kernel(tc, x, h_dn, xg1, xg2, adj, W_u, b_u, W_c
             w_rows.append(rows)
         h_rows = sbuf.tile([P, NODES], BF16, name="h_rows")
         nc.sync.dma_start(out=h_rows[:], in_=h_dn.rearrange("b o n -> (b o) n"))
+        bias = []
+        for g, b in enumerate((b_u, b_c)):
+            col = sbuf.tile([P, 1], BF16, name="bias%d" % g)
+            nc.sync.dma_start(out=col[:], in_=b.rearrange("(p o) -> p o", o=1))
+            bias.append(col)
+
+        half_copy = (nc.vector.tensor_copy, nc.scalar.copy)
+
+        z1 = [mx_operand(sbuf, "z1_%d" % h, HALF) for h in range(2)]
+        for h in range(2):
+            half_copy[h](
+                out=z1[h][0][:].rearrange("p (n t) -> p n t", t=4)[:, :, 0:2],
+                in_=xg2_rows[:].rearrange("p (j n) -> p n j", j=2)[:, HALF * h : HALF * (h + 1), :],
+            )
 
         xg2_t = mx_operand(sbuf, "xg2_t", 2 * P)
         xg2_words = xg2_rows[:].bitcast(F32)
         bank = work.tile([P, 4, P], F32, name="xg2_bank", tag="work")
         flip(nc, bank, [xg2_words[:, P * s : P * (s + 1)] for s in range(4)], ident_f32)
-        interleave(nc.scalar.copy, xg2_t, bank)
+        interleave(nc.vector.tensor_copy, xg2_t, bank)
         quantise(nc, xg2_t, 0, 2 * P)
-
-        z1_bank = []
-        for q in range(4):
-            zb = joined.tile([P, 4, QUARTER], F32, name="z1_bank%d" % q)
-            for j in range(2):
-                nc.tensor.matmul(
-                    out=zb[:, j, :],
-                    lhsT=ident_bf16[:],
-                    rhs=xg2_rows[:, NODES * j + QUARTER * q : NODES * j + QUARTER * (q + 1)],
-                    start=True,
-                    stop=True,
-                )
-            z1_bank.append(zb)
 
         adj_t = []
         for h in range(2):
@@ -122,12 +116,31 @@ def tile_gcgrucell_epsilon_pb_s_kernel(tc, x, h_dn, xg1, xg2, adj, W_u, b_u, W_c
             quantise(nc, operand, 0, HALF)
             adj_t.append(operand)
 
-        z0 = mx_operand(sbuf, "z0", NODES)
-        nc.vector.tensor_copy(
-            out=z0[0][:].rearrange("p (c i t) -> p c t i", i=4, t=4),
-            in_=early_rows[:].rearrange("p (t c i) -> p c t i", t=4, i=4),
-        )
-        quantise(nc, z0, 0, NODES)
+        for h in range(2):
+            xg3 = hop_psum.tile([P, 2, HALF], F32, name="xg3_%d" % h)
+            for j in range(2):
+                nc.tensor.matmul_mx(
+                    out=xg3[:, j, :],
+                    lhsT=xg2_t[1][:, P * j : P * (j + 1)].bitcast(FP8X4),
+                    lhsT_scale=xg2_t[2][:, P * j : P * (j + 1)],
+                    rhs=adj_t[h][1][:].bitcast(FP8X4),
+                    rhs_scale=adj_t[h][2][:],
+                    start=True,
+                    stop=True,
+                )
+            half_copy[h](
+                out=z1[h][0][:].rearrange("p (n t) -> p n t", t=4)[:, :, 2:4],
+                in_=xg3[:].rearrange("p j n -> p n j"),
+            )
+            quantise(nc, z1[h], 0, HALF)
+
+        z0 = [mx_operand(sbuf, "z0_%d" % h, HALF) for h in range(2)]
+        for h in range(2):
+            nc.vector.tensor_copy(
+                out=z0[h][0][:].rearrange("p (c i t) -> p c t i", i=4, t=4),
+                in_=early_rows[:].rearrange("p (t c i) -> p c t i", t=4, i=4)[:, 64 * h : 64 * (h + 1), :, :],
+            )
+            quantise(nc, z0[h], 0, HALF)
 
         w_t = []
         for g in range(2):
@@ -140,53 +153,30 @@ def tile_gcgrucell_epsilon_pb_s_kernel(tc, x, h_dn, xg1, xg2, adj, W_u, b_u, W_c
             quantise(nc, operand, 0, 2 * P)
             w_t.append(operand)
 
-        for q in range(4):
-            cols = slice(QUARTER * (q % 2), QUARTER * (q % 2 + 1))
-            for j in range(2):
-                nc.tensor.matmul_mx(
-                    out=z1_bank[q][:, 2 + j, :],
-                    lhsT=xg2_t[1][:, P * j : P * (j + 1)].bitcast(FP8X4),
-                    lhsT_scale=xg2_t[2][:, P * j : P * (j + 1)],
-                    rhs=adj_t[q // 2][1][:, cols].bitcast(FP8X4),
-                    rhs_scale=adj_t[q // 2][2][:, cols],
-                    start=True,
-                    stop=True,
-                )
-
-        def gate_pass(acc, g, k_pass, operand, h):
+        def gate_pass(acc, g, k_pass, operand):
             nc.tensor.matmul_mx(
                 out=acc[:],
                 lhsT=w_t[g][1][:, P * k_pass : P * (k_pass + 1)].bitcast(FP8X4),
                 lhsT_scale=w_t[g][2][:, P * k_pass : P * (k_pass + 1)],
-                rhs=operand[1][:, HALF * h : HALF * (h + 1)].bitcast(FP8X4),
-                rhs_scale=operand[2][:, HALF * h : HALF * (h + 1)],
+                rhs=operand[1][:].bitcast(FP8X4),
+                rhs_scale=operand[2][:],
                 start=(k_pass == 0),
                 stop=(k_pass == 1),
             )
 
-        gate = {}
-        for h in range(2):
-            for g in range(2):
-                gate[g, h] = work.tile([P, HALF], F32, name="gate%d%d" % (g, h), tag="work")
-                gate_pass(gate[g, h], g, 0, z0, h)
-
-        z1 = mx_operand(sbuf, "z1", NODES)
         out_rows = out.rearrange("b o n -> (b o) n")
         for h in range(2):
-            for q in (2 * h, 2 * h + 1):
-                copy = nc.scalar.copy if q % 2 == 0 else nc.vector.tensor_copy
-                copy(
-                    out=z1[0][:, 4 * QUARTER * q : 4 * QUARTER * (q + 1)].rearrange("p (n t) -> p n t", t=4),
-                    in_=z1_bank[q][:].rearrange("p t n -> p n t"),
-                )
-            quantise(nc, z1, HALF * h, HALF)
-            for g in (1, 0):
-                gate_pass(gate[g, h], g, 1, z1, h)
+            gate = []
+            for g in range(2):
+                acc = work.tile([P, HALF], F32, name="gate%d%d" % (g, h), tag="work")
+                gate_pass(acc, g, 0, z0[h])
+                gate_pass(acc, g, 1, z1[h])
+                gate.append(acc)
             cols = slice(HALF * h, HALF * (h + 1))
             cand = sbuf.tile([P, HALF], F32, name="cand%d" % h)
-            nc.scalar.activation(out=cand[:], in_=gate[1, h][:], func=ACT.Tanh, bias=bias[1][:], scale=1.0)
+            nc.scalar.activation(out=cand[:], in_=gate[1][:], func=ACT.Tanh, bias=bias[1][:], scale=1.0)
             upd = sbuf.tile([P, HALF], F32, name="upd%d" % h)
-            nc.scalar.activation(out=upd[:], in_=gate[0, h][:], func=ACT.Sigmoid, bias=bias[0][:], scale=1.0)
+            nc.scalar.activation(out=upd[:], in_=gate[0][:], func=ACT.Sigmoid, bias=bias[0][:], scale=1.0)
             diff = sbuf.tile([P, HALF], F32, name="diff%d" % h)
             nc.vector.tensor_tensor(out=diff[:], in0=h_rows[:, cols], in1=cand[:], op=ALU.subtract)
             prod = sbuf.tile([P, HALF], F32, name="prod%d" % h)

@@ -55,14 +55,12 @@ def tile_gcgrucell_epsilon_pb_s_kernel(tc, x, h_dn, xg1, xg2, adj, W_u, b_u, W_c
         sbuf = ctx.enter_context(tc.tile_pool(name="sbuf", bufs=1))
         hop_psum = ctx.enter_context(tc.psum_pool(name="hop_psum", bufs=1))
         work = ctx.enter_context(tc.psum_pool(name="work", bufs=4))
+        ctx.enter_context(tc.manual_schedule())
 
-        ident_f32 = sbuf.tile([P, P], F32, name="ident_f32")
-        masks.make_identity(nc, ident_f32[:])
-        warm_in = sbuf.tile([P, 1], F32, name="warm_in")
-        warm_out = sbuf.tile([P, 1], F32, name="warm_out")
-        nc.vector.memset(warm_in[:], 0.0)
-        nc.scalar.activation(out=warm_out[:], in_=warm_in[:], func=ACT.Sigmoid)
-
+        early_rows = sbuf.tile([P, 4 * NODES], BF16, name="early_rows")
+        nc.scalar.dma_start(out=early_rows[0:32, :], in_=x.rearrange("b (p j) n -> p (b j n)", j=4))
+        nc.scalar.dma_start(out=early_rows[64:128, :], in_=xg1.rearrange("b (p j) n -> p (b j n)", j=4))
+        nc.scalar.dma_start(out=early_rows[32:64, :], in_=h_dn.rearrange("b (p j) n -> p (b j n)", j=4))
         xg2_rows = sbuf.tile([P, 2 * NODES], BF16, name="xg2_rows")
         nc.sync.dma_start(out=xg2_rows[:], in_=xg2.rearrange("b (p j) v -> p (b j v)", j=2))
         adj_rows = []
@@ -73,50 +71,52 @@ def tile_gcgrucell_epsilon_pb_s_kernel(tc, x, h_dn, xg1, xg2, adj, W_u, b_u, W_c
                 in_=adj[HALF * h : HALF * (h + 1), :].rearrange("(i p) v -> p i v", p=P),
             )
             adj_rows.append(rows)
-        early_rows = sbuf.tile([P, 4 * NODES], BF16, name="early_rows")
-        nc.scalar.dma_start(out=early_rows[64:128, :], in_=xg1.rearrange("b (p j) n -> p (b j n)", j=4))
-        nc.sync.dma_start(out=early_rows[0:32, :], in_=x.rearrange("b (p j) n -> p (b j n)", j=4))
-        nc.sync.dma_start(out=early_rows[32:64, :], in_=h_dn.rearrange("b (p j) n -> p (b j n)", j=4))
         w_rows = []
-        for g, w in enumerate((W_u, W_c)):
+        for g, w in enumerate((W_c, W_u)):
             rows = sbuf.tile([P, KC], BF16, name="w_rows%d" % g)
             nc.sync.dma_start(out=rows[:], in_=w)
             w_rows.append(rows)
         h_rows = sbuf.tile([P, NODES], BF16, name="h_rows")
         nc.sync.dma_start(out=h_rows[:], in_=h_dn.rearrange("b o n -> (b o) n"))
         bias = []
-        for g, b in enumerate((b_u, b_c)):
+        for g, b in enumerate((b_c, b_u)):
             col = sbuf.tile([P, 1], BF16, name="bias%d" % g)
             nc.sync.dma_start(out=col[:], in_=b.rearrange("(p o) -> p o", o=1))
             bias.append(col)
 
-        half_copy = (nc.vector.tensor_copy, nc.scalar.copy)
-
-        z1 = [mx_operand(sbuf, "z1_%d" % h, HALF) for h in range(2)]
-        for h in range(2):
-            half_copy[h](
-                out=z1[h][0][:].rearrange("p (n t) -> p n t", t=4)[:, :, 0:2],
-                in_=xg2_rows[:].rearrange("p (j n) -> p n j", j=2)[:, HALF * h : HALF * (h + 1), :],
-            )
+        ident_f32 = sbuf.tile([P, P], F32, name="ident_f32")
+        masks.make_identity(nc, ident_f32[:])
+        warm_in = sbuf.tile([P, 1], F32, name="warm_in")
+        warm_out = sbuf.tile([P, 1], F32, name="warm_out")
+        nc.vector.memset(warm_in[:], 0.0)
+        nc.scalar.activation(out=warm_out[:], in_=warm_in[:], func=ACT.Sigmoid)
 
         xg2_t = mx_operand(sbuf, "xg2_t", 2 * P)
-        xg2_words = xg2_rows[:].bitcast(F32)
-        bank = work.tile([P, 4, P], F32, name="xg2_bank", tag="work")
-        flip(nc, bank, [xg2_words[:, P * s : P * (s + 1)] for s in range(4)], ident_f32)
-        interleave(nc.vector.tensor_copy, xg2_t, bank)
-        quantise(nc, xg2_t, 0, 2 * P)
+        adj_t = [mx_operand(sbuf, "adj_t%d" % h, HALF) for h in range(2)]
+        w_t = [mx_operand(sbuf, "w_t%d" % g, 2 * P) for g in range(2)]
+        z0 = [mx_operand(sbuf, "z0_%d" % h, HALF) for h in range(2)]
+        z1 = [mx_operand(sbuf, "z1_%d" % h, HALF) for h in range(2)]
 
-        adj_t = []
-        for h in range(2):
-            operand = mx_operand(sbuf, "adj_t%d" % h, HALF)
-            adj_words = adj_rows[h][:].bitcast(F32)
-            bank = work.tile([P, 4, P], F32, name="adj_bank%d" % h, tag="work")
-            flip(nc, bank, [adj_words[:, P * s : P * (s + 1)] for s in range(4)], ident_f32)
-            interleave(nc.scalar.copy, operand, bank)
-            quantise(nc, operand, 0, HALF)
-            adj_t.append(operand)
+        def flip_words(name, blocks):
+            bank = work.tile([P, 4, P], F32, name=name, tag="work")
+            flip(nc, bank, blocks, ident_f32)
+            return bank
 
-        for h in range(2):
+        def quarters(rows):
+            words = rows[:].bitcast(F32)
+            return [words[:, P * s : P * (s + 1)] for s in range(4)]
+
+        def weight_blocks(rows):
+            words = rows[:].bitcast(F32)
+            return [words[:, 0:256:2], words[:, 1:256:2], words[:, 256:384], words[:, 384:512]]
+
+        def group_z0(h):
+            nc.vector.tensor_copy(
+                out=z0[h][0][:].rearrange("p (c i t) -> p c t i", i=4, t=4),
+                in_=early_rows[:].rearrange("p (t c i) -> p c t i", t=4, i=4)[:, 64 * h : 64 * (h + 1), :, :],
+            )
+
+        def hop(h):
             xg3 = hop_psum.tile([P, 2, HALF], F32, name="xg3_%d" % h)
             for j in range(2):
                 nc.tensor.matmul_mx(
@@ -128,30 +128,7 @@ def tile_gcgrucell_epsilon_pb_s_kernel(tc, x, h_dn, xg1, xg2, adj, W_u, b_u, W_c
                     start=True,
                     stop=True,
                 )
-            half_copy[h](
-                out=z1[h][0][:].rearrange("p (n t) -> p n t", t=4)[:, :, 2:4],
-                in_=xg3[:].rearrange("p j n -> p n j"),
-            )
-            quantise(nc, z1[h], 0, HALF)
-
-        z0 = [mx_operand(sbuf, "z0_%d" % h, HALF) for h in range(2)]
-        for h in range(2):
-            nc.vector.tensor_copy(
-                out=z0[h][0][:].rearrange("p (c i t) -> p c t i", i=4, t=4),
-                in_=early_rows[:].rearrange("p (t c i) -> p c t i", t=4, i=4)[:, 64 * h : 64 * (h + 1), :, :],
-            )
-            quantise(nc, z0[h], 0, HALF)
-
-        w_t = []
-        for g in range(2):
-            operand = mx_operand(sbuf, "w_t%d" % g, 2 * P)
-            w_words = w_rows[g][:].bitcast(F32)
-            blocks = [w_words[:, 0:256:2], w_words[:, 1:256:2], w_words[:, 256:384], w_words[:, 384:512]]
-            bank = work.tile([P, 4, P], F32, name="w_bank%d" % g, tag="work")
-            flip(nc, bank, blocks, ident_f32)
-            interleave(nc.scalar.copy, operand, bank)
-            quantise(nc, operand, 0, 2 * P)
-            w_t.append(operand)
+            return xg3
 
         def gate_pass(acc, g, k_pass, operand):
             nc.tensor.matmul_mx(
@@ -164,23 +141,60 @@ def tile_gcgrucell_epsilon_pb_s_kernel(tc, x, h_dn, xg1, xg2, adj, W_u, b_u, W_c
                 stop=(k_pass == 1),
             )
 
+        for h in range(2):
+            nc.scalar.copy(
+                out=z1[h][0][:].rearrange("p (n t) -> p n t", t=4)[:, :, 0:2],
+                in_=xg2_rows[:].rearrange("p (j n) -> p n j", j=2)[:, HALF * h : HALF * (h + 1), :],
+            )
+        xg2_bank = flip_words("xg2_bank", quarters(xg2_rows))
+        interleave(nc.vector.tensor_copy, xg2_t, xg2_bank)
+        group_z0(0)
+        quantise(nc, xg2_t, 0, 2 * P)
+
+        for h in range(2):
+            adj_bank = flip_words("adj_bank%d" % h, quarters(adj_rows[h]))
+            interleave(nc.scalar.copy, adj_t[h], adj_bank)
+            quantise(nc, adj_t[h], 0, HALF)
+        for g in range(2):
+            w_bank = flip_words("w_bank%d" % g, weight_blocks(w_rows[g]))
+            interleave(nc.scalar.copy, w_t[g], w_bank)
+        group_z0(1)
+        for h in range(2):
+            quantise(nc, z0[h], 0, HALF)
+            quantise(nc, w_t[h], 0, 2 * P)
+
+        xg3 = [hop(h) for h in range(2)]
+        gate = {}
+        for g in range(2):
+            for h in range(2):
+                gate[g, h] = work.tile([P, HALF], F32, name="gate%d%d" % (g, h), tag="work")
+                gate_pass(gate[g, h], g, 0, z0[h])
+
+        upd = [sbuf.tile([P, HALF], F32, name="upd%d" % h) for h in range(2)]
+        cand = [sbuf.tile([P, HALF], F32, name="cand%d" % h) for h in range(2)]
+        for h in range(2):
+            nc.scalar.copy(
+                out=z1[h][0][:].rearrange("p (n t) -> p n t", t=4)[:, :, 2:4],
+                in_=xg3[h][:].rearrange("p j n -> p n j"),
+            )
+            quantise(nc, z1[h], 0, HALF)
+        for h in range(2):
+            for g in range(2):
+                gate_pass(gate[g, h], g, 1, z1[h])
+            nc.scalar.activation(out=cand[h][:], in_=gate[0, h][:], func=ACT.Tanh, bias=bias[0][:], scale=1.0)
+            nc.scalar.activation(out=upd[h][:], in_=gate[1, h][:], func=ACT.Sigmoid, bias=bias[1][:], scale=1.0)
+
         out_rows = out.rearrange("b o n -> (b o) n")
         for h in range(2):
-            gate = []
-            for g in range(2):
-                acc = work.tile([P, HALF], F32, name="gate%d%d" % (g, h), tag="work")
-                gate_pass(acc, g, 0, z0[h])
-                gate_pass(acc, g, 1, z1[h])
-                gate.append(acc)
-            cols = slice(HALF * h, HALF * (h + 1))
-            cand = sbuf.tile([P, HALF], F32, name="cand%d" % h)
-            nc.scalar.activation(out=cand[:], in_=gate[1][:], func=ACT.Tanh, bias=bias[1][:], scale=1.0)
-            upd = sbuf.tile([P, HALF], F32, name="upd%d" % h)
-            nc.scalar.activation(out=upd[:], in_=gate[0][:], func=ACT.Sigmoid, bias=bias[0][:], scale=1.0)
             diff = sbuf.tile([P, HALF], F32, name="diff%d" % h)
-            nc.vector.tensor_tensor(out=diff[:], in0=h_rows[:, cols], in1=cand[:], op=ALU.subtract)
             prod = sbuf.tile([P, HALF], F32, name="prod%d" % h)
-            nc.vector.tensor_tensor(out=prod[:], in0=upd[:], in1=diff[:], op=ALU.mult)
             res = sbuf.tile([P, HALF], F32, name="res%d" % h)
-            nc.vector.tensor_tensor(out=res[:], in0=prod[:], in1=cand[:], op=ALU.add)
-            nc.sync.dma_start(out=out_rows[:, cols], in_=res[:])
+            h_half = h_rows[:, HALF * h : HALF * (h + 1)]
+            ranges = [slice(QUARTER * r, QUARTER * (r + 1)) for r in range(2)]
+            for r in ranges:
+                nc.vector.tensor_tensor(out=diff[:, r], in0=h_half[:, r], in1=cand[h][:, r], op=ALU.subtract)
+            for r in ranges:
+                nc.vector.tensor_tensor(out=prod[:, r], in0=upd[h][:, r], in1=diff[:, r], op=ALU.mult)
+            for r in ranges:
+                nc.vector.tensor_tensor(out=res[:, r], in0=prod[:, r], in1=cand[h][:, r], op=ALU.add)
+            nc.sync.dma_start(out=out_rows[:, HALF * h : HALF * (h + 1)], in_=res[:])

@@ -66,10 +66,7 @@ def tile_gcgrucell_epsilon_pb_s_kernel(tc, x, h_dn, xg1, xg2, adj, W_u, b_u, W_c
         adj_rows = []
         for h in range(2):
             rows = sbuf.tile([P, 2 * NODES], BF16, name="adj_rows%d" % h)
-            nc.sync.dma_start(
-                out=rows[:].rearrange("p (i v) -> p i v", i=2),
-                in_=adj[HALF * h : HALF * (h + 1), :].rearrange("(i p) v -> p i v", p=P),
-            )
+            nc.sync.dma_start(out=rows[:], in_=adj[HALF * h : HALF * (h + 1), :].rearrange("(p i) v -> p (i v)", i=2))
             adj_rows.append(rows)
         w_rows = []
         for g, w in enumerate((W_c, W_u)):
@@ -142,33 +139,31 @@ def tile_gcgrucell_epsilon_pb_s_kernel(tc, x, h_dn, xg1, xg2, adj, W_u, b_u, W_c
             )
 
         for h in range(2):
-            nc.scalar.copy(
+            nc.vector.tensor_copy(
                 out=z1[h][0][:].rearrange("p (n t) -> p n t", t=4)[:, :, 0:2],
                 in_=xg2_rows[:].rearrange("p (j n) -> p n j", j=2)[:, HALF * h : HALF * (h + 1), :],
             )
         xg2_bank = flip_words("xg2_bank", quarters(xg2_rows))
-        interleave(nc.vector.tensor_copy, xg2_t, xg2_bank)
+        interleave(nc.scalar.copy, xg2_t, xg2_bank)
         group_z0(0)
         quantise(nc, xg2_t, 0, 2 * P)
 
         for h in range(2):
             adj_bank = flip_words("adj_bank%d" % h, quarters(adj_rows[h]))
-            interleave(nc.scalar.copy, adj_t[h], adj_bank)
+            nc.scalar.copy(
+                out=adj_t[h][0][:].bitcast(F32).rearrange("p (m i u) -> p m i u", i=2, u=2),
+                in_=adj_bank[:].rearrange("p (i u) m -> p m i u", u=2),
+            )
             quantise(nc, adj_t[h], 0, HALF)
         for g in range(2):
             w_bank = flip_words("w_bank%d" % g, weight_blocks(w_rows[g]))
             interleave(nc.scalar.copy, w_t[g], w_bank)
         group_z0(1)
-        for h in range(2):
-            quantise(nc, z0[h], 0, HALF)
-            quantise(nc, w_t[h], 0, 2 * P)
+        quantise(nc, z0[0], 0, HALF)
+        for g in range(2):
+            quantise(nc, w_t[g], 0, 2 * P)
 
         xg3 = [hop(h) for h in range(2)]
-        gate = {}
-        for g in range(2):
-            for h in range(2):
-                gate[g, h] = work.tile([P, HALF], F32, name="gate%d%d" % (g, h), tag="work")
-                gate_pass(gate[g, h], g, 0, z0[h])
 
         upd = [sbuf.tile([P, HALF], F32, name="upd%d" % h) for h in range(2)]
         cand = [sbuf.tile([P, HALF], F32, name="cand%d" % h) for h in range(2)]
@@ -177,12 +172,17 @@ def tile_gcgrucell_epsilon_pb_s_kernel(tc, x, h_dn, xg1, xg2, adj, W_u, b_u, W_c
                 out=z1[h][0][:].rearrange("p (n t) -> p n t", t=4)[:, :, 2:4],
                 in_=xg3[h][:].rearrange("p j n -> p n j"),
             )
-            quantise(nc, z1[h], 0, HALF)
+        quantise(nc, z1[0], 0, HALF)
+        quantise(nc, z0[1], 0, HALF)
+        quantise(nc, z1[1], 0, HALF)
         for h in range(2):
+            gate = [work.tile([P, HALF], F32, name="gate%d%d" % (g, h), tag="work") for g in range(2)]
             for g in range(2):
-                gate_pass(gate[g, h], g, 1, z1[h])
-            nc.scalar.activation(out=cand[h][:], in_=gate[0, h][:], func=ACT.Tanh, bias=bias[0][:], scale=1.0)
-            nc.scalar.activation(out=upd[h][:], in_=gate[1, h][:], func=ACT.Sigmoid, bias=bias[1][:], scale=1.0)
+                gate_pass(gate[g], g, 0, z0[h])
+            for g in range(2):
+                gate_pass(gate[g], g, 1, z1[h])
+            nc.scalar.activation(out=cand[h][:], in_=gate[0][:], func=ACT.Tanh, bias=bias[0][:], scale=1.0)
+            nc.scalar.activation(out=upd[h][:], in_=gate[1][:], func=ACT.Sigmoid, bias=bias[1][:], scale=1.0)
 
         out_rows = out.rearrange("b o n -> (b o) n")
         for h in range(2):

@@ -55,7 +55,6 @@ def tile_gcgrucell_epsilon_pb_s_kernel(tc, x, h_dn, xg1, xg2, adj, W_u, b_u, W_c
         sbuf = ctx.enter_context(tc.tile_pool(name="sbuf", bufs=1))
         hop_psum = ctx.enter_context(tc.psum_pool(name="hop_psum", bufs=1))
         work = ctx.enter_context(tc.psum_pool(name="work", bufs=4))
-        ctx.enter_context(tc.manual_schedule())
 
         early_rows = sbuf.tile([P, 4 * NODES], BF16, name="early_rows")
         nc.scalar.dma_start(out=early_rows[0:32, :], in_=x.rearrange("b (p j) n -> p (b j n)", j=4))

@@ -27,24 +27,14 @@ def mx_operand(pool, name, columns):
     return grouped, codes, scales
 
 
-def quantise(nc, operand, first, count):
+def quantise(nc, operand):
     grouped, codes, scales = operand
-    nc.vector.quantize_mx(
-        out=codes[:, first : first + count].bitcast(FP8X4),
-        scales=scales[:, first : first + count],
-        in_=grouped[:, 4 * first : 4 * (first + count)],
-    )
-
-
-def flip(nc, bank, blocks, ident):
-    for s in range(4):
-        nc.tensor.transpose(bank[:, s, :], blocks[s], ident[:])
+    nc.vector.quantize_mx(out=codes[:].bitcast(FP8X4), scales=scales[:], in_=grouped[:])
 
 
 def interleave(copy, operand, bank):
-    grouped = operand[0]
     copy(
-        out=grouped[:].bitcast(F32).rearrange("p (a m u) -> p a m u", a=2, u=2),
+        out=operand[0][:].bitcast(F32).rearrange("p (a m u) -> p a m u", a=2, u=2),
         in_=bank[:].rearrange("p (a u) m -> p a m u", u=2),
     )
 
@@ -54,31 +44,36 @@ def tile_gcgrucell_epsilon_pb_s_kernel(tc, x, h_dn, xg1, xg2, adj, W_u, b_u, W_c
     with ExitStack() as ctx:
         sbuf = ctx.enter_context(tc.tile_pool(name="sbuf", bufs=1))
         hop_psum = ctx.enter_context(tc.psum_pool(name="hop_psum", bufs=1))
-        work = ctx.enter_context(tc.psum_pool(name="work", bufs=4))
+        work = ctx.enter_context(tc.psum_pool(name="work", bufs=6))
+        ctx.enter_context(tc.manual_schedule())
 
         early_rows = sbuf.tile([P, 4 * NODES], BF16, name="early_rows")
-        nc.scalar.dma_start(out=early_rows[0:32, :], in_=x.rearrange("b (p j) n -> p (b j n)", j=4))
-        nc.scalar.dma_start(out=early_rows[64:128, :], in_=xg1.rearrange("b (p j) n -> p (b j n)", j=4))
-        nc.scalar.dma_start(out=early_rows[32:64, :], in_=h_dn.rearrange("b (p j) n -> p (b j n)", j=4))
         xg2_rows = sbuf.tile([P, 2 * NODES], BF16, name="xg2_rows")
-        nc.sync.dma_start(out=xg2_rows[:], in_=xg2.rearrange("b (p j) v -> p (b j v)", j=2))
-        adj_rows = []
-        for h in range(2):
-            rows = sbuf.tile([P, 2 * NODES], BF16, name="adj_rows%d" % h)
-            nc.sync.dma_start(out=rows[:], in_=adj[HALF * h : HALF * (h + 1), :].rearrange("(p i) v -> p (i v)", i=2))
-            adj_rows.append(rows)
-        w_rows = []
-        for g, w in enumerate((W_c, W_u)):
-            rows = sbuf.tile([P, KC], BF16, name="w_rows%d" % g)
-            nc.sync.dma_start(out=rows[:], in_=w)
-            w_rows.append(rows)
+        adj_rows = [sbuf.tile([P, 2 * NODES], BF16, name="adj_rows%d" % h) for h in range(2)]
+        w_rows = [sbuf.tile([P, KC], BF16, name="w_rows%d" % g) for g in range(2)]
         h_rows = sbuf.tile([P, NODES], BF16, name="h_rows")
+        bias = [sbuf.tile([P, 1], BF16, name="bias%d" % g) for g in range(2)]
+
+        def load_z0(q):
+            q.dma_start(out=early_rows[0:32, :], in_=x.rearrange("b (p j) n -> p (b j n)", j=4))
+            q.dma_start(out=early_rows[64:128, :], in_=xg1.rearrange("b (p j) n -> p (b j n)", j=4))
+            q.dma_start(out=early_rows[32:64, :], in_=h_dn.rearrange("b (p j) n -> p (b j n)", j=4))
+
+        def load_adj(h):
+            nc.sync.dma_start(out=adj_rows[h][:], in_=adj[HALF * h : HALF * (h + 1), :].rearrange("(p i) v -> p (i v)", i=2))
+
+        def load_w(g):
+            nc.sync.dma_start(out=w_rows[g][:], in_=(W_c, W_u)[g])
+
+        nc.sync.dma_start(out=xg2_rows[:], in_=xg2.rearrange("b (p j) v -> p (b j v)", j=2))
+        load_z0(nc.sync)
+        load_adj(0)
+        load_adj(1)
+        load_w(0)
+        load_w(1)
         nc.sync.dma_start(out=h_rows[:], in_=h_dn.rearrange("b o n -> (b o) n"))
-        bias = []
         for g, b in enumerate((b_c, b_u)):
-            col = sbuf.tile([P, 1], BF16, name="bias%d" % g)
-            nc.sync.dma_start(out=col[:], in_=b.rearrange("(p o) -> p o", o=1))
-            bias.append(col)
+            nc.sync.dma_start(out=bias[g][:], in_=b.rearrange("(p o) -> p o", o=1))
 
         ident_f32 = sbuf.tile([P, P], F32, name="ident_f32")
         masks.make_identity(nc, ident_f32[:])
@@ -93,9 +88,10 @@ def tile_gcgrucell_epsilon_pb_s_kernel(tc, x, h_dn, xg1, xg2, adj, W_u, b_u, W_c
         z0 = [mx_operand(sbuf, "z0_%d" % h, HALF) for h in range(2)]
         z1 = [mx_operand(sbuf, "z1_%d" % h, HALF) for h in range(2)]
 
-        def flip_words(name, blocks):
+        def flip(name, blocks):
             bank = work.tile([P, 4, P], F32, name=name, tag="work")
-            flip(nc, bank, blocks, ident_f32)
+            for s in range(4):
+                nc.tensor.transpose(bank[:, s, :], blocks[s], ident_f32[:])
             return bank
 
         def quarters(rows):
@@ -112,6 +108,18 @@ def tile_gcgrucell_epsilon_pb_s_kernel(tc, x, h_dn, xg1, xg2, adj, W_u, b_u, W_c
                 in_=early_rows[:].rearrange("p (t c i) -> p c t i", t=4, i=4)[:, 64 * h : 64 * (h + 1), :, :],
             )
 
+        def place_xg2(copy, h):
+            copy(
+                out=z1[h][0][:].rearrange("p (n t) -> p n t", t=4)[:, :, 0:2],
+                in_=xg2_rows[:].rearrange("p (j n) -> p n j", j=2)[:, HALF * h : HALF * (h + 1), :],
+            )
+
+        def copy_adj(copy, h, bank):
+            copy(
+                out=adj_t[h][0][:].bitcast(F32).rearrange("p (m i u) -> p m i u", i=2, u=2),
+                in_=bank[:].rearrange("p (i u) m -> p m i u", u=2),
+            )
+
         def hop(h):
             xg3 = hop_psum.tile([P, 2, HALF], F32, name="xg3_%d" % h)
             for j in range(2):
@@ -126,6 +134,12 @@ def tile_gcgrucell_epsilon_pb_s_kernel(tc, x, h_dn, xg1, xg2, adj, W_u, b_u, W_c
                 )
             return xg3
 
+        def place_xg3(copy, h, xg3):
+            copy(
+                out=z1[h][0][:].rearrange("p (n t) -> p n t", t=4)[:, :, 2:4],
+                in_=xg3[:].rearrange("p j n -> p n j"),
+            )
+
         def gate_pass(acc, g, k_pass, operand):
             nc.tensor.matmul_mx(
                 out=acc[:],
@@ -137,63 +151,85 @@ def tile_gcgrucell_epsilon_pb_s_kernel(tc, x, h_dn, xg1, xg2, adj, W_u, b_u, W_c
                 stop=(k_pass == 1),
             )
 
-        for h in range(2):
-            nc.vector.tensor_copy(
-                out=z1[h][0][:].rearrange("p (n t) -> p n t", t=4)[:, :, 0:2],
-                in_=xg2_rows[:].rearrange("p (j n) -> p n j", j=2)[:, HALF * h : HALF * (h + 1), :],
-            )
-        xg2_bank = flip_words("xg2_bank", quarters(xg2_rows))
-        interleave(nc.scalar.copy, xg2_t, xg2_bank)
-        group_z0(0)
-        quantise(nc, xg2_t, 0, 2 * P)
-
-        for h in range(2):
-            adj_bank = flip_words("adj_bank%d" % h, quarters(adj_rows[h]))
-            nc.scalar.copy(
-                out=adj_t[h][0][:].bitcast(F32).rearrange("p (m i u) -> p m i u", i=2, u=2),
-                in_=adj_bank[:].rearrange("p (i u) m -> p m i u", u=2),
-            )
-            quantise(nc, adj_t[h], 0, HALF)
-        for g in range(2):
-            w_bank = flip_words("w_bank%d" % g, weight_blocks(w_rows[g]))
-            interleave(nc.scalar.copy, w_t[g], w_bank)
-        group_z0(1)
-        quantise(nc, z0[0], 0, HALF)
-        for g in range(2):
-            quantise(nc, w_t[g], 0, 2 * P)
-
-        xg3 = [hop(h) for h in range(2)]
-
         upd = [sbuf.tile([P, HALF], F32, name="upd%d" % h) for h in range(2)]
         cand = [sbuf.tile([P, HALF], F32, name="cand%d" % h) for h in range(2)]
-        for h in range(2):
-            nc.scalar.copy(
-                out=z1[h][0][:].rearrange("p (n t) -> p n t", t=4)[:, :, 2:4],
-                in_=xg3[h][:].rearrange("p j n -> p n j"),
-            )
-        quantise(nc, z1[0], 0, HALF)
-        quantise(nc, z0[1], 0, HALF)
-        quantise(nc, z1[1], 0, HALF)
-        for h in range(2):
-            gate = [work.tile([P, HALF], F32, name="gate%d%d" % (g, h), tag="work") for g in range(2)]
-            for g in range(2):
-                gate_pass(gate[g], g, 0, z0[h])
-            for g in range(2):
-                gate_pass(gate[g], g, 1, z1[h])
-            nc.scalar.activation(out=cand[h][:], in_=gate[0][:], func=ACT.Tanh, bias=bias[0][:], scale=1.0)
-            nc.scalar.activation(out=upd[h][:], in_=gate[1][:], func=ACT.Sigmoid, bias=bias[1][:], scale=1.0)
+        diff = [sbuf.tile([P, HALF], F32, name="diff%d" % h) for h in range(2)]
+        prod = [sbuf.tile([P, HALF], F32, name="prod%d" % h) for h in range(2)]
+        res = [sbuf.tile([P, HALF], F32, name="res%d" % h) for h in range(2)]
+        whole = [slice(0, HALF)]
+        parts = [slice(QUARTER * r, QUARTER * (r + 1)) for r in range(2)]
+
+        def candidate(h, acc, ranges):
+            for r in ranges:
+                nc.scalar.activation(out=cand[h][:, r], in_=acc[:, r], func=ACT.Tanh, bias=bias[0][:], scale=1.0)
+
+        def update(h, acc, ranges):
+            for r in ranges:
+                nc.scalar.activation(out=upd[h][:, r], in_=acc[:, r], func=ACT.Sigmoid, bias=bias[1][:], scale=1.0)
 
         out_rows = out.rearrange("b o n -> (b o) n")
-        for h in range(2):
-            diff = sbuf.tile([P, HALF], F32, name="diff%d" % h)
-            prod = sbuf.tile([P, HALF], F32, name="prod%d" % h)
-            res = sbuf.tile([P, HALF], F32, name="res%d" % h)
+
+        def blend_diff(h, ranges):
             h_half = h_rows[:, HALF * h : HALF * (h + 1)]
-            ranges = [slice(QUARTER * r, QUARTER * (r + 1)) for r in range(2)]
             for r in ranges:
-                nc.vector.tensor_tensor(out=diff[:, r], in0=h_half[:, r], in1=cand[h][:, r], op=ALU.subtract)
+                nc.vector.tensor_tensor(out=diff[h][:, r], in0=h_half[:, r], in1=cand[h][:, r], op=ALU.subtract)
+
+        def blend_prod(h, ranges):
             for r in ranges:
-                nc.vector.tensor_tensor(out=prod[:, r], in0=upd[h][:, r], in1=diff[:, r], op=ALU.mult)
+                nc.vector.tensor_tensor(out=prod[h][:, r], in0=upd[h][:, r], in1=diff[h][:, r], op=ALU.mult)
+
+        def blend_sum(h, ranges):
             for r in ranges:
-                nc.vector.tensor_tensor(out=res[:, r], in0=prod[:, r], in1=cand[h][:, r], op=ALU.add)
-            nc.sync.dma_start(out=out_rows[:, HALF * h : HALF * (h + 1)], in_=res[:])
+                nc.vector.tensor_tensor(out=res[h][:, r], in0=prod[h][:, r], in1=cand[h][:, r], op=ALU.add)
+
+        def store(h):
+            nc.sync.dma_start(out=out_rows[:, HALF * h : HALF * (h + 1)], in_=res[h][:])
+
+        place_xg2(nc.scalar.copy, 0)
+        xg2_bank = flip("xg2_bank", quarters(xg2_rows))
+        interleave(nc.scalar.copy, xg2_t, xg2_bank)
+        place_xg2(nc.scalar.copy, 1)
+        group_z0(0)
+        quantise(nc, xg2_t)
+        group_z0(1)
+        quantise(nc, z0[0])
+        adj0_bank = flip("adj0_bank", quarters(adj_rows[0]))
+        copy_adj(nc.scalar.copy, 0, adj0_bank)
+        quantise(nc, z0[1])
+        quantise(nc, adj_t[0])
+        adj1_bank = flip("adj1_bank", quarters(adj_rows[1]))
+        copy_adj(nc.scalar.copy, 1, adj1_bank)
+        quantise(nc, adj_t[1])
+        wc_bank = flip("wc_bank", weight_blocks(w_rows[0]))
+        interleave(nc.scalar.copy, w_t[0], wc_bank)
+        quantise(nc, w_t[0])
+        xg3_0 = hop(0)
+        xg3_1 = hop(1)
+        place_xg3(nc.scalar.copy, 0, xg3_0)
+        place_xg3(nc.vector.tensor_copy, 1, xg3_1)
+        wu_bank = flip("wu_bank", weight_blocks(w_rows[1]))
+        interleave(nc.scalar.copy, w_t[1], wu_bank)
+        quantise(nc, z1[0])
+        quantise(nc, w_t[1])
+        quantise(nc, z1[1])
+        gate = [[work.tile([P, HALF], F32, name="gate%d%d" % (g, h), tag="work") for h in range(2)] for g in range(2)]
+        gate_pass(gate[0][0], 0, 0, z0[0])
+        gate_pass(gate[0][1], 0, 0, z0[1])
+        gate_pass(gate[0][0], 0, 1, z1[0])
+        gate_pass(gate[1][0], 1, 0, z0[0])
+        gate_pass(gate[1][0], 1, 1, z1[0])
+        gate_pass(gate[0][1], 0, 1, z1[1])
+        gate_pass(gate[1][1], 1, 0, z0[1])
+        gate_pass(gate[1][1], 1, 1, z1[1])
+        candidate(0, gate[0][0], whole)
+        update(0, gate[1][0], whole)
+        candidate(1, gate[0][1], whole)
+        update(1, gate[1][1], parts)
+        blend_diff(0, whole)
+        blend_prod(0, whole)
+        blend_diff(1, whole)
+        blend_sum(0, whole)
+        store(0)
+        blend_prod(1, parts)
+        blend_sum(1, parts)
+        store(1)

@@ -88,6 +88,11 @@ def tile_gcgrucell_epsilon_pb_s_kernel(tc, x, h_dn, xg1, xg2, adj, W_u, b_u, W_c
         z0 = [mx_operand(sbuf, "z0_%d" % h, HALF) for h in range(2)]
         z1 = [mx_operand(sbuf, "z1_%d" % h, HALF) for h in range(2)]
 
+        def warm_up(name, count):
+            bank = work.tile([P, P], F32, name=name, tag="work")
+            for i in range(count):
+                nc.tensor.matmul(bank[:], lhsT=ident_f32[:], rhs=ident_f32[:], start=True, stop=True)
+
         def flip(name, blocks):
             bank = work.tile([P, 4, P], F32, name=name, tag="work")
             for s in range(4):
@@ -185,42 +190,40 @@ def tile_gcgrucell_epsilon_pb_s_kernel(tc, x, h_dn, xg1, xg2, adj, W_u, b_u, W_c
         def store(h):
             nc.sync.dma_start(out=out_rows[:, HALF * h : HALF * (h + 1)], in_=res[h][:])
 
-        place_xg2(nc.scalar.copy, 0)
+        warm_up("warm_head", 3)
+        place_xg2(nc.vector.tensor_copy, 0)
+        place_xg2(nc.vector.tensor_copy, 1)
         xg2_bank = flip("xg2_bank", quarters(xg2_rows))
+        warm_up("warm_mid", 2)
         interleave(nc.scalar.copy, xg2_t, xg2_bank)
-        place_xg2(nc.scalar.copy, 1)
         group_z0(0)
         quantise(nc, xg2_t)
         group_z0(1)
         quantise(nc, z0[0])
         adj0_bank = flip("adj0_bank", quarters(adj_rows[0]))
         copy_adj(nc.scalar.copy, 0, adj0_bank)
-        quantise(nc, z0[1])
         quantise(nc, adj_t[0])
         adj1_bank = flip("adj1_bank", quarters(adj_rows[1]))
         copy_adj(nc.scalar.copy, 1, adj1_bank)
+        quantise(nc, z0[1])
         quantise(nc, adj_t[1])
         wc_bank = flip("wc_bank", weight_blocks(w_rows[0]))
-        interleave(nc.scalar.copy, w_t[0], wc_bank)
-        quantise(nc, w_t[0])
+        wu_bank = flip("wu_bank", weight_blocks(w_rows[1]))
         xg3_0 = hop(0)
         xg3_1 = hop(1)
+        interleave(nc.scalar.copy, w_t[0], wc_bank)
+        quantise(nc, w_t[0])
+        interleave(nc.vector.tensor_copy, w_t[1], wu_bank)
         place_xg3(nc.scalar.copy, 0, xg3_0)
-        place_xg3(nc.vector.tensor_copy, 1, xg3_1)
-        wu_bank = flip("wu_bank", weight_blocks(w_rows[1]))
-        interleave(nc.scalar.copy, w_t[1], wu_bank)
+        place_xg3(nc.scalar.copy, 1, xg3_1)
         quantise(nc, z1[0])
         quantise(nc, w_t[1])
         quantise(nc, z1[1])
         gate = [[work.tile([P, HALF], F32, name="gate%d%d" % (g, h), tag="work") for h in range(2)] for g in range(2)]
-        gate_pass(gate[0][0], 0, 0, z0[0])
-        gate_pass(gate[0][1], 0, 0, z0[1])
-        gate_pass(gate[0][0], 0, 1, z1[0])
-        gate_pass(gate[1][0], 1, 0, z0[0])
-        gate_pass(gate[1][0], 1, 1, z1[0])
-        gate_pass(gate[0][1], 0, 1, z1[1])
-        gate_pass(gate[1][1], 1, 0, z0[1])
-        gate_pass(gate[1][1], 1, 1, z1[1])
+        for h in range(2):
+            for g in range(2):
+                gate_pass(gate[g][h], g, 0, z0[h])
+                gate_pass(gate[g][h], g, 1, z1[h])
         candidate(0, gate[0][0], whole)
         update(0, gate[1][0], whole)
         candidate(1, gate[0][1], whole)

@@ -55,9 +55,9 @@ def tile_gcgrucell_epsilon_pb_s_kernel(tc, x, h_dn, xg1, xg2, adj, W_u, b_u, W_c
         bias = [sbuf.tile([P, 1], BF16, name="bias%d" % g) for g in range(2)]
 
         def load_z0(q):
-            q.dma_start(out=early_rows[0:32, :], in_=x.rearrange("b (p j) n -> p (b j n)", j=4))
-            q.dma_start(out=early_rows[64:128, :], in_=xg1.rearrange("b (p j) n -> p (b j n)", j=4))
-            q.dma_start(out=early_rows[32:64, :], in_=h_dn.rearrange("b (p j) n -> p (b j n)", j=4))
+            q.dma_start(out=early_rows[0:64, 0 : 2 * NODES], in_=x.rearrange("b (p e) n -> p (b e n)", e=2))
+            q.dma_start(out=early_rows[64:128, 0 : 2 * NODES], in_=h_dn.rearrange("b (p e) n -> p (b e n)", e=2))
+            q.dma_start(out=early_rows[:, 2 * NODES : 4 * NODES], in_=xg1.rearrange("b (p e) n -> p (b e n)", e=2))
 
         def load_adj(h):
             nc.sync.dma_start(out=adj_rows[h][:], in_=adj[HALF * h : HALF * (h + 1), :].rearrange("(p i) v -> p (i v)", i=2))
@@ -66,10 +66,10 @@ def tile_gcgrucell_epsilon_pb_s_kernel(tc, x, h_dn, xg1, xg2, adj, W_u, b_u, W_c
             nc.sync.dma_start(out=w_rows[g][:], in_=(W_c, W_u)[g])
 
         nc.sync.dma_start(out=xg2_rows[:], in_=xg2.rearrange("b (p j) v -> p (b j v)", j=2))
-        load_z0(nc.sync)
         load_adj(0)
         load_adj(1)
         load_w(0)
+        load_z0(nc.sync)
         load_w(1)
         nc.sync.dma_start(out=h_rows[:], in_=h_dn.rearrange("b o n -> (b o) n"))
         for g, b in enumerate((b_c, b_u)):
@@ -102,10 +102,6 @@ def tile_gcgrucell_epsilon_pb_s_kernel(tc, x, h_dn, xg1, xg2, adj, W_u, b_u, W_c
         def quarters(rows):
             words = rows[:].bitcast(F32)
             return [words[:, P * s : P * (s + 1)] for s in range(4)]
-
-        def weight_blocks(rows):
-            words = rows[:].bitcast(F32)
-            return [words[:, 0:256:2], words[:, 1:256:2], words[:, 256:384], words[:, 384:512]]
 
         def group_z0(h):
             nc.vector.tensor_copy(
@@ -194,36 +190,38 @@ def tile_gcgrucell_epsilon_pb_s_kernel(tc, x, h_dn, xg1, xg2, adj, W_u, b_u, W_c
         place_xg2(nc.vector.tensor_copy, 0)
         place_xg2(nc.vector.tensor_copy, 1)
         xg2_bank = flip("xg2_bank", quarters(xg2_rows))
-        warm_up("warm_mid", 2)
         interleave(nc.scalar.copy, xg2_t, xg2_bank)
-        group_z0(0)
         quantise(nc, xg2_t)
-        group_z0(1)
-        quantise(nc, z0[0])
         adj0_bank = flip("adj0_bank", quarters(adj_rows[0]))
         copy_adj(nc.scalar.copy, 0, adj0_bank)
         quantise(nc, adj_t[0])
         adj1_bank = flip("adj1_bank", quarters(adj_rows[1]))
         copy_adj(nc.scalar.copy, 1, adj1_bank)
-        quantise(nc, z0[1])
         quantise(nc, adj_t[1])
-        wc_bank = flip("wc_bank", weight_blocks(w_rows[0]))
-        wu_bank = flip("wu_bank", weight_blocks(w_rows[1]))
+        wc_bank = flip("wc_bank", quarters(w_rows[0]))
+        interleave(nc.scalar.copy, w_t[0], wc_bank)
+        warm_up("warm_mid", 2)
         xg3_0 = hop(0)
         xg3_1 = hop(1)
-        interleave(nc.scalar.copy, w_t[0], wc_bank)
+        group_z0(0)
         quantise(nc, w_t[0])
-        interleave(nc.vector.tensor_copy, w_t[1], wu_bank)
+        quantise(nc, z0[0])
+        wu_bank = flip("wu_bank", quarters(w_rows[1]))
         place_xg3(nc.scalar.copy, 0, xg3_0)
-        place_xg3(nc.scalar.copy, 1, xg3_1)
         quantise(nc, z1[0])
+        interleave(nc.scalar.copy, w_t[1], wu_bank)
+        place_xg3(nc.scalar.copy, 1, xg3_1)
+        group_z0(1)
         quantise(nc, w_t[1])
+        quantise(nc, z0[1])
         quantise(nc, z1[1])
         gate = [[work.tile([P, HALF], F32, name="gate%d%d" % (g, h), tag="work") for h in range(2)] for g in range(2)]
-        for h in range(2):
+        for g in range(2):
+            gate_pass(gate[g][0], g, 0, z0[0])
+            gate_pass(gate[g][0], g, 1, z1[0])
+        for k_pass, operand in enumerate((z0[1], z1[1])):
             for g in range(2):
-                gate_pass(gate[g][h], g, 0, z0[h])
-                gate_pass(gate[g][h], g, 1, z1[h])
+                gate_pass(gate[g][1], g, k_pass, operand)
         candidate(0, gate[0][0], whole)
         update(0, gate[1][0], whole)
         candidate(1, gate[0][1], whole)

@@ -207,6 +207,7 @@ def tile_gcgrucell_epsilon_pb_s_kernel(tc, x, h_dn, xg1, xg2, adj, W_u, b_u, W_c
         quantise(nc, w_t[0])
         quantise(nc, z0[0])
         wu_bank = flip("wu_bank", quarters(w_rows[1]))
+        warm_up("warm_hop", 1)
         place_xg3(nc.scalar.copy, 0, xg3_0)
         quantise(nc, z1[0])
         interleave(nc.scalar.copy, w_t[1], wu_bank)
@@ -216,9 +217,11 @@ def tile_gcgrucell_epsilon_pb_s_kernel(tc, x, h_dn, xg1, xg2, adj, W_u, b_u, W_c
         quantise(nc, z0[1])
         quantise(nc, z1[1])
         gate = [[work.tile([P, HALF], F32, name="gate%d%d" % (g, h), tag="work") for h in range(2)] for g in range(2)]
-        for g in range(2):
-            gate_pass(gate[g][0], g, 0, z0[0])
-            gate_pass(gate[g][0], g, 1, z1[0])
+        gate_pass(gate[0][0], 0, 0, z0[0])
+        gate_pass(gate[0][0], 0, 1, z1[0])
+        warm_up("warm_gates", 1)
+        gate_pass(gate[1][0], 1, 0, z0[0])
+        gate_pass(gate[1][0], 1, 1, z1[0])
         for k_pass, operand in enumerate((z0[1], z1[1])):
             for g in range(2):
                 gate_pass(gate[g][1], g, k_pass, operand)

@@ -183,8 +183,9 @@ def tile_gcgrucell_epsilon_pb_s_kernel(tc, x, h_dn, xg1, xg2, adj, W_u, b_u, W_c
             for r in ranges:
                 nc.vector.tensor_tensor(out=res[h][:, r], in0=prod[h][:, r], in1=cand[h][:, r], op=ALU.add)
 
-        def store(h):
-            nc.sync.dma_start(out=out_rows[:, HALF * h : HALF * (h + 1)], in_=res[h][:])
+        def store(h, ranges):
+            for r in ranges:
+                nc.sync.dma_start(out=out_rows[:, HALF * h : HALF * (h + 1)][:, r], in_=res[h][:, r])
 
         warm_up("warm_head", 3)
         place_xg2(nc.vector.tensor_copy, 0)
@@ -233,7 +234,7 @@ def tile_gcgrucell_epsilon_pb_s_kernel(tc, x, h_dn, xg1, xg2, adj, W_u, b_u, W_c
         blend_prod(0, whole)
         blend_diff(1, whole)
         blend_sum(0, whole)
-        store(0)
+        store(0, whole)
         blend_prod(1, parts)
         blend_sum(1, parts)
-        store(1)
+        store(1, parts)

from contextlib import ExitStack

import concourse.masks as masks
import concourse.mybir as mybir

F32 = mybir.dt.float32
BF16 = mybir.dt.bfloat16
U32 = mybir.dt.uint32
U8 = mybir.dt.uint8
FP8X4 = mybir.dt.float8_e4m3fn_x4
ACT = mybir.ActivationFunctionType
ALU = mybir.AluOpType

P = 128
NODES = 512
HALF = NODES // 2
QUARTER = NODES // 4
KC = 1024

FLOPS = 2 * 256 * NODES * NODES + 2 * 2 * P * KC * NODES


def mx_operand(pool, name, columns):
    grouped = pool.tile([P, 4 * columns], BF16, name=name + "_grouped", align_bytes=64)
    codes = pool.tile([P, columns], U32, name=name + "_codes", align_bytes=64)
    scales = pool.tile([P, columns], U8, name=name + "_scales", align_bytes=64)
    return grouped, codes, scales


def quantise(nc, operand):
    grouped, codes, scales = operand
    nc.vector.quantize_mx(out=codes[:].bitcast(FP8X4), scales=scales[:], in_=grouped[:])


def interleave(copy, operand, bank):
    copy(
        out=operand[0][:].bitcast(F32).rearrange("p (a m u) -> p a m u", a=2, u=2),
        in_=bank[:].rearrange("p (a u) m -> p a m u", u=2),
    )


def tile_gcgrucell_epsilon_pb_s_kernel(tc, x, h_dn, xg1, xg2, adj, W_u, b_u, W_c, b_c, out):
    nc = tc.nc
    with ExitStack() as ctx:
        sbuf = ctx.enter_context(tc.tile_pool(name="sbuf", bufs=1))
        hop_psum = ctx.enter_context(tc.psum_pool(name="hop_psum", bufs=1))
        work = ctx.enter_context(tc.psum_pool(name="work", bufs=6))
        ctx.enter_context(tc.manual_schedule())

        early_rows = sbuf.tile([P, 4 * NODES], BF16, name="early_rows")
        xg2_rows = sbuf.tile([P, 2 * NODES], BF16, name="xg2_rows")
        adj_rows = [sbuf.tile([P, 2 * NODES], BF16, name="adj_rows%d" % h) for h in range(2)]
        w_rows = [sbuf.tile([P, KC], BF16, name="w_rows%d" % g) for g in range(2)]
        h_rows = sbuf.tile([P, NODES], BF16, name="h_rows")
        bias = [sbuf.tile([P, 1], BF16, name="bias%d" % g) for g in range(2)]

        def load_z0(q):
            q.dma_start(out=early_rows[0:64, 0 : 2 * NODES], in_=x.rearrange("b (p e) n -> p (b e n)", e=2))
            q.dma_start(out=early_rows[64:128, 0 : 2 * NODES], in_=h_dn.rearrange("b (p e) n -> p (b e n)", e=2))
            q.dma_start(out=early_rows[:, 2 * NODES : 4 * NODES], in_=xg1.rearrange("b (p e) n -> p (b e n)", e=2))

        def load_adj(h):
            nc.sync.dma_start(out=adj_rows[h][:], in_=adj[HALF * h : HALF * (h + 1), :].rearrange("(p i) v -> p (i v)", i=2))

        def load_w(g):
            nc.sync.dma_start(out=w_rows[g][:], in_=(W_c, W_u)[g])

        nc.sync.dma_start(out=xg2_rows[:], in_=xg2.rearrange("b (p j) v -> p (b j v)", j=2))
        load_adj(0)
        load_adj(1)
        load_w(0)
        load_z0(nc.sync)
        load_w(1)
        nc.sync.dma_start(out=h_rows[:], in_=h_dn.rearrange("b o n -> (b o) n"))
        for g, b in enumerate((b_c, b_u)):
            nc.sync.dma_start(out=bias[g][:], in_=b.rearrange("(p o) -> p o", o=1))

        ident_f32 = sbuf.tile([P, P], F32, name="ident_f32")
        masks.make_identity(nc, ident_f32[:])
        warm_in = sbuf.tile([P, 1], F32, name="warm_in")
        warm_out = sbuf.tile([P, 1], F32, name="warm_out")
        nc.vector.memset(warm_in[:], 0.0)
        nc.scalar.activation(out=warm_out[:], in_=warm_in[:], func=ACT.Sigmoid)

        xg2_t = mx_operand(sbuf, "xg2_t", 2 * P)
        adj_t = [mx_operand(sbuf, "adj_t%d" % h, HALF) for h in range(2)]
        w_t = [mx_operand(sbuf, "w_t%d" % g, 2 * P) for g in range(2)]
        z0 = [mx_operand(sbuf, "z0_%d" % h, HALF) for h in range(2)]
        z1 = [mx_operand(sbuf, "z1_%d" % h, HALF) for h in range(2)]

        def warm_up(name, count):
            bank = work.tile([P, P], F32, name=name, tag="work")
            for i in range(count):
                nc.tensor.matmul(bank[:], lhsT=ident_f32[:], rhs=ident_f32[:], start=True, stop=True)

        def flip(name, blocks):
            bank = work.tile([P, 4, P], F32, name=name, tag="work")
            for s in range(4):
                nc.tensor.transpose(bank[:, s, :], blocks[s], ident_f32[:])
            return bank

        def quarters(rows):
            words = rows[:].bitcast(F32)
            return [words[:, P * s : P * (s + 1)] for s in range(4)]

        def group_z0(h):
            nc.vector.tensor_copy(
                out=z0[h][0][:].rearrange("p (c i t) -> p c t i", i=4, t=4),
                in_=early_rows[:].rearrange("p (t c i) -> p c t i", t=4, i=4)[:, 64 * h : 64 * (h + 1), :, :],
            )

        def place_xg2(copy, h):
            copy(
                out=z1[h][0][:].rearrange("p (n t) -> p n t", t=4)[:, :, 0:2],
                in_=xg2_rows[:].rearrange("p (j n) -> p n j", j=2)[:, HALF * h : HALF * (h + 1), :],
            )

        def copy_adj(copy, h, bank):
            copy(
                out=adj_t[h][0][:].bitcast(F32).rearrange("p (m i u) -> p m i u", i=2, u=2),
                in_=bank[:].rearrange("p (i u) m -> p m i u", u=2),
            )

        def hop(h):
            xg3 = hop_psum.tile([P, 2, HALF], F32, name="xg3_%d" % h)
            for j in range(2):
                nc.tensor.matmul_mx(
                    out=xg3[:, j, :],
                    lhsT=xg2_t[1][:, P * j : P * (j + 1)].bitcast(FP8X4),
                    lhsT_scale=xg2_t[2][:, P * j : P * (j + 1)],
                    rhs=adj_t[h][1][:].bitcast(FP8X4),
                    rhs_scale=adj_t[h][2][:],
                    start=True,
                    stop=True,
                )
            return xg3

        def place_xg3(copy, h, xg3):
            copy(
                out=z1[h][0][:].rearrange("p (n t) -> p n t", t=4)[:, :, 2:4],
                in_=xg3[:].rearrange("p j n -> p n j"),
            )

        def gate_pass(acc, g, k_pass, operand):
            nc.tensor.matmul_mx(
                out=acc[:],
                lhsT=w_t[g][1][:, P * k_pass : P * (k_pass + 1)].bitcast(FP8X4),
                lhsT_scale=w_t[g][2][:, P * k_pass : P * (k_pass + 1)],
                rhs=operand[1][:].bitcast(FP8X4),
                rhs_scale=operand[2][:],
                start=(k_pass == 0),
                stop=(k_pass == 1),
            )

        upd = [sbuf.tile([P, HALF], F32, name="upd%d" % h) for h in range(2)]
        cand = [sbuf.tile([P, HALF], F32, name="cand%d" % h) for h in range(2)]
        diff = [sbuf.tile([P, HALF], F32, name="diff%d" % h) for h in range(2)]
        prod = [sbuf.tile([P, HALF], F32, name="prod%d" % h) for h in range(2)]
        res = [sbuf.tile([P, HALF], F32, name="res%d" % h) for h in range(2)]
        whole = [slice(0, HALF)]
        parts = [slice(QUARTER * r, QUARTER * (r + 1)) for r in range(2)]

        def candidate(h, acc, ranges):
            for r in ranges:
                nc.scalar.activation(out=cand[h][:, r], in_=acc[:, r], func=ACT.Tanh, bias=bias[0][:], scale=1.0)

        def update(h, acc, ranges):
            for r in ranges:
                nc.scalar.activation(out=upd[h][:, r], in_=acc[:, r], func=ACT.Sigmoid, bias=bias[1][:], scale=1.0)

        out_rows = out.rearrange("b o n -> (b o) n")

        def blend_diff(h, ranges):
            h_half = h_rows[:, HALF * h : HALF * (h + 1)]
            for r in ranges:
                nc.vector.tensor_tensor(out=diff[h][:, r], in0=h_half[:, r], in1=cand[h][:, r], op=ALU.subtract)

        def blend_prod(h, ranges):
            for r in ranges:
                nc.vector.tensor_tensor(out=prod[h][:, r], in0=upd[h][:, r], in1=diff[h][:, r], op=ALU.mult)

        def blend_sum(h, ranges):
            for r in ranges:
                nc.vector.tensor_tensor(out=res[h][:, r], in0=prod[h][:, r], in1=cand[h][:, r], op=ALU.add)

        def store(h, ranges):
            for r in ranges:
                nc.sync.dma_start(out=out_rows[:, HALF * h : HALF * (h + 1)][:, r], in_=res[h][:, r])

        warm_up("warm_head", 3)
        place_xg2(nc.vector.tensor_copy, 0)
        place_xg2(nc.vector.tensor_copy, 1)
        xg2_bank = flip("xg2_bank", quarters(xg2_rows))
        interleave(nc.scalar.copy, xg2_t, xg2_bank)
        quantise(nc, xg2_t)
        adj0_bank = flip("adj0_bank", quarters(adj_rows[0]))
        copy_adj(nc.scalar.copy, 0, adj0_bank)
        quantise(nc, adj_t[0])
        adj1_bank = flip("adj1_bank", quarters(adj_rows[1]))
        copy_adj(nc.scalar.copy, 1, adj1_bank)
        quantise(nc, adj_t[1])
        wc_bank = flip("wc_bank", quarters(w_rows[0]))
        interleave(nc.scalar.copy, w_t[0], wc_bank)
        warm_up("warm_mid", 2)
        xg3_0 = hop(0)
        xg3_1 = hop(1)
        group_z0(0)
        quantise(nc, w_t[0])
        quantise(nc, z0[0])
        wu_bank = flip("wu_bank", quarters(w_rows[1]))
        warm_up("warm_hop", 1)
        place_xg3(nc.scalar.copy, 0, xg3_0)
        quantise(nc, z1[0])
        interleave(nc.scalar.copy, w_t[1], wu_bank)
        place_xg3(nc.scalar.copy, 1, xg3_1)
        group_z0(1)
        quantise(nc, w_t[1])
        quantise(nc, z0[1])
        quantise(nc, z1[1])
        gate = [[work.tile([P, HALF], F32, name="gate%d%d" % (g, h), tag="work") for h in range(2)] for g in range(2)]
        gate_pass(gate[0][0], 0, 0, z0[0])
        gate_pass(gate[0][0], 0, 1, z1[0])
        warm_up("warm_gates", 1)
        gate_pass(gate[1][0], 1, 0, z0[0])
        gate_pass(gate[1][0], 1, 1, z1[0])
        for k_pass, operand in enumerate((z0[1], z1[1])):
            for g in range(2):
                gate_pass(gate[g][1], g, k_pass, operand)
        candidate(0, gate[0][0], whole)
        update(0, gate[1][0], whole)
        candidate(1, gate[0][1], whole)
        update(1, gate[1][1], parts)
        blend_diff(0, whole)
        blend_prod(0, whole)
        blend_diff(1, whole)
        blend_sum(0, whole)
        store(0, whole)
        blend_prod(1, parts)
        blend_sum(1, parts)
        store(1, parts)
